import numpy as np
import ml_dtypes


def mxq(x, axis, fmt="e4m3"):
    dtype, down = {"e4m3": (ml_dtypes.float8_e4m3fn, 7), "e5m2": (ml_dtypes.float8_e5m2, 14)}[fmt]
    v = np.moveaxis(np.asarray(x, np.float32).astype(ml_dtypes.bfloat16).astype(np.float64), axis, -1)
    blocks = v.reshape(v.shape[:-1] + (-1, 32))
    amax = np.abs(blocks).max(-1, keepdims=True)
    byte = np.maximum(np.where(amax > 0, np.frexp(amax)[1] - 1 + 127, 0) - down, 1)
    scale = np.exp2(byte - 127.0)
    codes = (blocks / scale).astype(np.float32).astype(dtype).astype(np.float64)
    return np.moveaxis((codes * scale).reshape(v.shape), -1, axis)


WIDE = False


def mx_kscale(k):
    if not WIDE:
        return np.ones(k)
    levels = np.array([10, -10, 5, -5, 0])
    a = np.random.permutation(np.resize(levels, k // 512 * 4)).reshape(k // 512, 4)
    idx = np.arange(k)
    return np.exp2(a[idx // 512, idx % 128 // 32])


BF16 = ml_dtypes.bfloat16


def bf(x):
    return np.asarray(x, np.float32).astype(BF16)


def f64(x):
    return np.asarray(x).astype(np.float64)


E2M1 = np.array([0.0, 0.5, 1.0, 1.5, 2.0, 3.0, 4.0, 6.0, -0.0, -0.5, -1.0, -1.5, -2.0, -3.0, -4.0, -6.0])


def pack_weight(w, fmt):
    k, n = w.shape
    w = f64(bf(w)).reshape(k // 32, 32, n)
    amax = np.abs(w).max(1)
    if fmt == "e4m3":
        byte = np.frexp(amax)[1] - 1 + 127 - 7
    else:
        mant, ex = np.frexp(amax / 6.0)
        byte = np.where(mant > 0.5, ex, ex - 1) + 127
    byte = np.clip(np.where(amax > 0, byte, 1), 1, 254)
    scaled = (w * np.exp2(127.0 - byte)[:, None, :]).reshape(k, n).astype(np.float32)
    by_word = np.ascontiguousarray(scaled.reshape(k // 512, 128, 4, n).transpose(0, 1, 3, 2))
    if fmt == "e4m3":
        words = by_word.astype(ml_dtypes.float8_e4m3fn).view(np.uint8)
    else:
        c = by_word.astype(ml_dtypes.float4_e2m1fn).view(np.uint8) & 0xF
        words = c[..., 0::2] | (c[..., 1::2] << 4)
    return np.ascontiguousarray(words), np.ascontiguousarray(byte.astype(np.uint8).reshape(k // 512, 16, n))


def unpack_weight(words, scales, fmt):
    g, p, n, _ = words.shape
    if fmt == "e4m3":
        vals = np.ascontiguousarray(words).view(ml_dtypes.float8_e4m3fn).astype(np.float64)
    else:
        nib = np.empty((g, p, n, 4), np.uint8)
        nib[..., 0::2] = words & 0xF
        nib[..., 1::2] = words >> 4
        vals = E2M1[nib]
    vals = vals * np.repeat(np.exp2(scales.astype(np.float64) - 127.0), 8, axis=1)[..., None]
    return vals.transpose(0, 1, 3, 2).reshape(g * 512, n)


B, N, D, H, DH, WS = 4, 1024, 1024, 4, 128, 512
INNER = H * DH
NW = N // WS
BW = B * NW
FMT = "e4m3"


def elu(u):
    return np.where(u > 0.0, u, np.exp(np.minimum(u, 0.0)) - 1.0)


def heads(t):
    return t.reshape(BW, WS, H, DH).transpose(0, 2, 1, 3)


def setup_inputs():
    s = mx_kscale(D)
    x = bf(np.random.standard_normal((B, N, D)) * s)
    k_words, k_scales = pack_weight(np.random.standard_normal((D, INNER)) / np.sqrt(D) / s[:, None], FMT)
    v_words, v_scales = pack_weight(np.random.standard_normal((D, INNER)) * 0.3 / np.sqrt(D * WS) / s[:, None], FMT)
    return {"x": x,
            "w_k_words": k_words, "w_k_scales": k_scales,
            "w_v_words": v_words, "w_v_scales": v_scales}


def reference(x, w_k_words, w_k_scales, w_v_words, w_v_scales):
    xq = mxq(f64(x).reshape(BW, WS, D), 2, "e4m3")
    k = heads(xq @ unpack_weight(w_k_words, w_k_scales, FMT))
    v = heads(xq @ unpack_weight(w_v_words, w_v_scales, FMT))
    kf = elu(k) + 1.0
    return mxq(kf, 2, "e4m3").transpose(0, 1, 3, 2) @ mxq(v, 2, "e4m3")

@@ -1,0 +1,192 @@
+from contextlib import ExitStack
+
+import concourse.mybir as mybir
+from concourse.masks import make_identity
+
+F32 = mybir.dt.float32
+BF16 = mybir.dt.bfloat16
+I32 = mybir.dt.int32
+U32 = mybir.dt.uint32
+U8 = mybir.dt.uint8
+FP8X4 = mybir.dt.float8_e4m3fn_x4
+ACT = mybir.ActivationFunctionType
+ALU = mybir.AluOpType
+
+P = 128
+PACK = 4
+K_PASS = P * PACK
+
+BATCH, TOKENS, FEATURES = 4, 1024, 1024
+WINDOW = 512
+WINDOWS = BATCH * TOKENS // WINDOW
+HEADS, HEAD_DIM = 4, 128
+INNER = HEADS * HEAD_DIM
+GROUPS = FEATURES // K_PASS
+TOKEN_TILES = WINDOW // P
+HALF_TILES = TOKEN_TILES // 2
+PAIRS = 2
+QUADRANTS = 4
+
+FLOPS = 2 * BATCH * TOKENS * FEATURES * 2 * INNER + 2 * WINDOWS * HEADS * WINDOW * HEAD_DIM * HEAD_DIM
+
+
+def tile_localcontextprocessor_pa_t_kernel(
+    tc, x, w_k_words, w_k_scales, w_v_words, w_v_scales, out
+):
+    nc = tc.nc
+    x_windows = x.rearrange("b (j p t) d -> (b j) p t d", p=P, t=TOKEN_TILES)
+
+    with ExitStack() as ctx:
+        ctx.enter_context(tc.manual_schedule())
+        keep = ctx.enter_context(tc.tile_pool(name="keep", bufs=1))
+        twice = ctx.enter_context(tc.tile_pool(name="twice", bufs=2))
+        heads = ctx.enter_context(tc.tile_pool(name="heads", bufs=4))
+        banks = ctx.enter_context(tc.psum_pool(name="banks", bufs=8))
+
+        w_planes = keep.tile([P, 2, GROUPS, INNER], U8, align_bytes=64)
+        nc.vector.memset(w_planes[:].bitcast(I32), 0)
+        identity = keep.tile([P, P], F32)
+        make_identity(nc, identity[:])
+
+        x_tiles = [
+            keep.tile([P, TOKEN_TILES, FEATURES], BF16, name="x_win%d" % w) for w in range(WINDOWS)
+        ]
+
+        def load_x(w):
+            for half in range(2):
+                tiles = slice(HALF_TILES * half, HALF_TILES * (half + 1))
+                nc.sync.dma_start(out=x_tiles[w][:, tiles, :], in_=x_windows[w, :, tiles, :])
+
+        w_words = keep.tile([P, 2, GROUPS, INNER * PACK], U8, align_bytes=64)
+
+        load_x(0)
+        load_x(1)
+        for kv, words in enumerate((w_k_words, w_v_words)):
+            nc.sync.dma_start(
+                out=w_words[:, kv, :, :].bitcast(I32),
+                in_=words.rearrange("g p n t -> p g (n t)").bitcast(I32),
+            )
+        for kv, scales in enumerate((w_k_scales, w_v_scales)):
+            for quadrant in range(QUADRANTS):
+                rows = slice(4 * quadrant, 4 * quadrant + 4)
+                nc.sync.dma_start(
+                    out=w_planes[32 * quadrant : 32 * quadrant + 4, kv, :, :].bitcast(I32),
+                    in_=scales[:, rows, :].rearrange("g r n -> r g n").bitcast(I32),
+                )
+        for w in range(2, WINDOWS):
+            load_x(w)
+
+        x_grouped, x_codes, x_planes = {}, {}, {}
+        kv_grouped, kv_codes, kv_planes = {}, {}, {}
+
+        def transpose_x(w):
+            x_grouped[w] = twice.tile(
+                [P, GROUPS, WINDOW, PACK], BF16, name="x_grouped", align_bytes=64
+            )
+            grouped_pairs = x_grouped[w][:].bitcast(F32)
+            x_pairs = x_tiles[w][:].bitcast(F32)
+            pairs_in_group = K_PASS // 2
+            for half in range(2):
+                for g in range(GROUPS):
+                    flipped = banks.tile([P, PAIRS, HALF_TILES * P], F32, tag="bank")
+                    for u in range(PAIRS):
+                        for s in range(HALF_TILES):
+                            nc.tensor.transpose(
+                                flipped[:, u, P * s : P * (s + 1)],
+                                x_pairs[
+                                    :,
+                                    HALF_TILES * half + s,
+                                    pairs_in_group * g + u : pairs_in_group * (g + 1) : PAIRS,
+                                ],
+                                identity[:],
+                            )
+                    columns = slice(HALF_TILES * P * half, HALF_TILES * P * (half + 1))
+                    nc.scalar.copy(
+                        out=grouped_pairs[:, g, columns, :],
+                        in_=flipped[:].rearrange("p u n -> p n u"),
+                    )
+
+        def quantise_x(w):
+            x_codes[w] = twice.tile([P, GROUPS, WINDOW], U32, name="x_codes", align_bytes=64)
+            x_planes[w] = twice.tile([P, GROUPS, WINDOW], U8, name="x_planes", align_bytes=64)
+            nc.vector.quantize_mx(
+                out=x_codes[w][:].rearrange("p g n -> p (g n)").bitcast(FP8X4),
+                scales=x_planes[w][:].rearrange("p g n -> p (g n)"),
+                in_=x_grouped[w][:].rearrange("p g n k -> p (g n k)"),
+            )
+
+        def project_head(w, kv, h):
+            product = banks.tile([P, TOKEN_TILES, HEAD_DIM], F32, tag="bank")
+            for t in range(TOKEN_TILES):
+                for g in range(GROUPS):
+                    nc.tensor.matmul_mx(
+                        out=product[:, t, :],
+                        lhsT=x_codes[w][:, g, P * t : P * (t + 1)].bitcast(FP8X4),
+                        lhsT_scale=x_planes[w][:, g, P * t : P * (t + 1)],
+                        rhs=w_words[
+                            :, kv, g, PACK * HEAD_DIM * h : PACK * HEAD_DIM * (h + 1)
+                        ].bitcast(FP8X4),
+                        rhs_scale=w_planes[:, kv, g, HEAD_DIM * h : HEAD_DIM * (h + 1)],
+                        start=(g == 0),
+                        stop=(g == GROUPS - 1),
+                    )
+            return product[:].rearrange("p t c -> p c t")
+
+        def project(w):
+            kv_grouped[w] = twice.tile(
+                [P, 2, HEADS, HEAD_DIM, PACK], BF16, name="kv_grouped", align_bytes=64
+            )
+            for h in range(HEADS):
+                k = project_head(w, 0, h)
+                v = project_head(w, 1, h)
+                exp_k = heads.tile([P, HEAD_DIM, PACK], F32, name="exp_k")
+                nc.scalar.activation(out=exp_k[:], in_=k, func=ACT.Exp)
+                nc.scalar.copy(out=kv_grouped[w][:, 1, h, :, :], in_=v)
+                nc.vector.tensor_scalar(
+                    out=exp_k[:], in0=exp_k[:], scalar1=1.0, scalar2=None, op0=ALU.min
+                )
+                nc.vector.scalar_tensor_tensor(
+                    out=kv_grouped[w][:, 0, h, :, :],
+                    in0=k,
+                    scalar=0.0,
+                    in1=exp_k[:],
+                    op0=ALU.max,
+                    op1=ALU.add,
+                )
+
+        def quantise_kv(w):
+            kv_codes[w] = twice.tile([P, 2, HEADS, HEAD_DIM], U32, name="kv_codes", align_bytes=64)
+            kv_planes[w] = twice.tile([P, 2, HEADS, HEAD_DIM], U8, name="kv_planes", align_bytes=64)
+            nc.vector.quantize_mx(
+                out=kv_codes[w][:].rearrange("p s h c -> p (s h c)").bitcast(FP8X4),
+                scales=kv_planes[w][:].rearrange("p s h c -> p (s h c)"),
+                in_=kv_grouped[w][:].rearrange("p s h c t -> p (s h c t)"),
+            )
+
+        def context(w):
+            product = banks.tile([P, HEADS, HEAD_DIM], F32, tag="bank")
+            for h in range(HEADS):
+                nc.tensor.matmul_mx(
+                    out=product[:, h, :],
+                    lhsT=kv_codes[w][:, 0, h, :].bitcast(FP8X4),
+                    lhsT_scale=kv_planes[w][:, 0, h, :],
+                    rhs=kv_codes[w][:, 1, h, :].bitcast(FP8X4),
+                    rhs_scale=kv_planes[w][:, 1, h, :],
+                    start=True,
+                    stop=True,
+                )
+            result = twice.tile([P, HEADS, HEAD_DIM], F32, name="result")
+            nc.vector.tensor_copy(out=result[:], in_=product[:])
+            nc.sync.dma_start(out=out[w].rearrange("h d e -> d h e"), in_=result[:])
+
+        for i in range(-1, WINDOWS + 1):
+            if i + 1 < WINDOWS:
+                transpose_x(i + 1)
+            if 0 <= i - 1:
+                quantise_kv(i - 1)
+            if i + 1 < WINDOWS:
+                quantise_x(i + 1)
+            if 0 <= i < WINDOWS:
+                project(i)
+            if 0 <= i - 1:
+                context(i - 1)

@@ -23,9 +23,12 @@ HEADS, HEAD_DIM = 4, 128
 INNER = HEADS * HEAD_DIM
 GROUPS = FEATURES // K_PASS
 TOKEN_TILES = WINDOW // P
-HALF_TILES = TOKEN_TILES // 2
+HALVES = 2
+HALF_TILES = TOKEN_TILES // HALVES
+HALF = HALF_TILES * P
 PAIRS = 2
 QUADRANTS = 4
+K, V = 0, 1
 
 FLOPS = 2 * BATCH * TOKENS * FEATURES * 2 * INNER + 2 * WINDOWS * HEADS * WINDOW * HEAD_DIM * HEAD_DIM
 
@@ -40,7 +43,7 @@ def tile_localcontextprocessor_pa_t_kernel(
         ctx.enter_context(tc.manual_schedule())
         keep = ctx.enter_context(tc.tile_pool(name="keep", bufs=1))
         twice = ctx.enter_context(tc.tile_pool(name="twice", bufs=2))
-        heads = ctx.enter_context(tc.tile_pool(name="heads", bufs=4))
+        four = ctx.enter_context(tc.tile_pool(name="four", bufs=4))
         banks = ctx.enter_context(tc.psum_pool(name="banks", bufs=8))
 
         w_planes = keep.tile([P, 2, GROUPS, INNER], U8, align_bytes=64)
@@ -53,76 +56,78 @@ def tile_localcontextprocessor_pa_t_kernel(
         ]
 
         def load_x(w):
-            for half in range(2):
+            for half in range(HALVES):
                 tiles = slice(HALF_TILES * half, HALF_TILES * (half + 1))
                 nc.sync.dma_start(out=x_tiles[w][:, tiles, :], in_=x_windows[w, :, tiles, :])
 
         w_words = keep.tile([P, 2, GROUPS, INNER * PACK], U8, align_bytes=64)
 
         load_x(0)
-        load_x(1)
-        for kv, words in enumerate((w_k_words, w_v_words)):
+        for kv, words in ((K, w_k_words), (V, w_v_words)):
             nc.sync.dma_start(
                 out=w_words[:, kv, :, :].bitcast(I32),
                 in_=words.rearrange("g p n t -> p g (n t)").bitcast(I32),
             )
-        for kv, scales in enumerate((w_k_scales, w_v_scales)):
+        for kv, scales in ((K, w_k_scales), (V, w_v_scales)):
             for quadrant in range(QUADRANTS):
                 rows = slice(4 * quadrant, 4 * quadrant + 4)
                 nc.sync.dma_start(
                     out=w_planes[32 * quadrant : 32 * quadrant + 4, kv, :, :].bitcast(I32),
                     in_=scales[:, rows, :].rearrange("g r n -> r g n").bitcast(I32),
                 )
-        for w in range(2, WINDOWS):
+        for w in range(1, WINDOWS):
             load_x(w)
 
         x_grouped, x_codes, x_planes = {}, {}, {}
         kv_grouped, kv_codes, kv_planes = {}, {}, {}
 
-        def transpose_x(w):
-            x_grouped[w] = twice.tile(
-                [P, GROUPS, WINDOW, PACK], BF16, name="x_grouped", align_bytes=64
+        def transpose_x(w, half):
+            x_grouped[w, half] = four.tile(
+                [P, GROUPS, HALF, PACK], BF16, name="x_grouped", align_bytes=64
             )
-            grouped_pairs = x_grouped[w][:].bitcast(F32)
+            grouped_pairs = x_grouped[w, half][:].bitcast(F32)
             x_pairs = x_tiles[w][:].bitcast(F32)
             pairs_in_group = K_PASS // 2
-            for half in range(2):
-                for g in range(GROUPS):
-                    flipped = banks.tile([P, PAIRS, HALF_TILES * P], F32, tag="bank")
-                    for u in range(PAIRS):
-                        for s in range(HALF_TILES):
-                            nc.tensor.transpose(
-                                flipped[:, u, P * s : P * (s + 1)],
-                                x_pairs[
-                                    :,
-                                    HALF_TILES * half + s,
-                                    pairs_in_group * g + u : pairs_in_group * (g + 1) : PAIRS,
-                                ],
-                                identity[:],
-                            )
-                    columns = slice(HALF_TILES * P * half, HALF_TILES * P * (half + 1))
-                    nc.scalar.copy(
-                        out=grouped_pairs[:, g, columns, :],
-                        in_=flipped[:].rearrange("p u n -> p n u"),
-                    )
+            for g in range(GROUPS):
+                flipped = banks.tile([P, PAIRS, HALF], F32, tag="bank")
+                for u in range(PAIRS):
+                    for s in range(HALF_TILES):
+                        nc.tensor.transpose(
+                            flipped[:, u, P * s : P * (s + 1)],
+                            x_pairs[
+                                :,
+                                HALF_TILES * half + s,
+                                pairs_in_group * g + u : pairs_in_group * (g + 1) : PAIRS,
+                            ],
+                            identity[:],
+                        )
+                nc.scalar.copy(
+                    out=grouped_pairs[:, g, :, :], in_=flipped[:].rearrange("p u n -> p n u")
+                )
 
-        def quantise_x(w):
-            x_codes[w] = twice.tile([P, GROUPS, WINDOW], U32, name="x_codes", align_bytes=64)
-            x_planes[w] = twice.tile([P, GROUPS, WINDOW], U8, name="x_planes", align_bytes=64)
+        def quantise_x(w, half):
+            if half == 0:
+                x_codes[w] = twice.tile(
+                    [P, HALVES, GROUPS, HALF], U32, name="x_codes", align_bytes=64
+                )
+                x_planes[w] = twice.tile(
+                    [P, HALVES, GROUPS, HALF], U8, name="x_planes", align_bytes=64
+                )
             nc.vector.quantize_mx(
-                out=x_codes[w][:].rearrange("p g n -> p (g n)").bitcast(FP8X4),
-                scales=x_planes[w][:].rearrange("p g n -> p (g n)"),
-                in_=x_grouped[w][:].rearrange("p g n k -> p (g n k)"),
+                out=x_codes[w][:, half, :, :].rearrange("p g n -> p (g n)").bitcast(FP8X4),
+                scales=x_planes[w][:, half, :, :].rearrange("p g n -> p (g n)"),
+                in_=x_grouped[w, half][:].rearrange("p g n k -> p (g n k)"),
             )
 
-        def project_head(w, kv, h):
+        def project(w, kv, h):
             product = banks.tile([P, TOKEN_TILES, HEAD_DIM], F32, tag="bank")
             for t in range(TOKEN_TILES):
+                half, tokens = t // HALF_TILES, slice(P * (t % HALF_TILES), P * (t % HALF_TILES + 1))
                 for g in range(GROUPS):
                     nc.tensor.matmul_mx(
                         out=product[:, t, :],
-                        lhsT=x_codes[w][:, g, P * t : P * (t + 1)].bitcast(FP8X4),
-                        lhsT_scale=x_planes[w][:, g, P * t : P * (t + 1)],
+                        lhsT=x_codes[w][:, half, g, tokens].bitcast(FP8X4),
+                        lhsT_scale=x_planes[w][:, half, g, tokens],
                         rhs=w_words[
                             :, kv, g, PACK * HEAD_DIM * h : PACK * HEAD_DIM * (h + 1)
                         ].bitcast(FP8X4),
@@ -132,35 +137,11 @@ def tile_localcontextprocessor_pa_t_kernel(
                     )
             return product[:].rearrange("p t c -> p c t")
 
-        def project(w):
-            kv_grouped[w] = twice.tile(
-                [P, 2, HEADS, HEAD_DIM, PACK], BF16, name="kv_grouped", align_bytes=64
-            )
-            for h in range(HEADS):
-                k = project_head(w, 0, h)
-                v = project_head(w, 1, h)
-                exp_k = heads.tile([P, HEAD_DIM, PACK], F32, name="exp_k")
-                nc.scalar.activation(out=exp_k[:], in_=k, func=ACT.Exp)
-                nc.scalar.copy(out=kv_grouped[w][:, 1, h, :, :], in_=v)
-                nc.vector.tensor_scalar(
-                    out=exp_k[:], in0=exp_k[:], scalar1=1.0, scalar2=None, op0=ALU.min
-                )
-                nc.vector.scalar_tensor_tensor(
-                    out=kv_grouped[w][:, 0, h, :, :],
-                    in0=k,
-                    scalar=0.0,
-                    in1=exp_k[:],
-                    op0=ALU.max,
-                    op1=ALU.add,
-                )
-
-        def quantise_kv(w):
-            kv_codes[w] = twice.tile([P, 2, HEADS, HEAD_DIM], U32, name="kv_codes", align_bytes=64)
-            kv_planes[w] = twice.tile([P, 2, HEADS, HEAD_DIM], U8, name="kv_planes", align_bytes=64)
+        def quantise_kv(w, h):
             nc.vector.quantize_mx(
-                out=kv_codes[w][:].rearrange("p s h c -> p (s h c)").bitcast(FP8X4),
-                scales=kv_planes[w][:].rearrange("p s h c -> p (s h c)"),
-                in_=kv_grouped[w][:].rearrange("p s h c t -> p (s h c t)"),
+                out=kv_codes[w][:, h, :, :].rearrange("p s c -> p (s c)").bitcast(FP8X4),
+                scales=kv_planes[w][:, h, :, :].rearrange("p s c -> p (s c)"),
+                in_=kv_grouped[w][:, h, :, :, :].rearrange("p s c t -> p (s c t)"),
             )
 
         def context(w):
@@ -168,10 +149,10 @@ def tile_localcontextprocessor_pa_t_kernel(
             for h in range(HEADS):
                 nc.tensor.matmul_mx(
                     out=product[:, h, :],
-                    lhsT=kv_codes[w][:, 0, h, :].bitcast(FP8X4),
-                    lhsT_scale=kv_planes[w][:, 0, h, :],
-                    rhs=kv_codes[w][:, 1, h, :].bitcast(FP8X4),
-                    rhs_scale=kv_planes[w][:, 1, h, :],
+                    lhsT=kv_codes[w][:, h, K, :].bitcast(FP8X4),
+                    lhsT_scale=kv_planes[w][:, h, K, :],
+                    rhs=kv_codes[w][:, h, V, :].bitcast(FP8X4),
+                    rhs_scale=kv_planes[w][:, h, V, :],
                     start=True,
                     stop=True,
                 )
@@ -179,14 +160,46 @@ def tile_localcontextprocessor_pa_t_kernel(
             nc.vector.tensor_copy(out=result[:], in_=product[:])
             nc.sync.dma_start(out=out[w].rearrange("h d e -> d h e"), in_=result[:])
 
-        for i in range(-1, WINDOWS + 1):
-            if i + 1 < WINDOWS:
-                transpose_x(i + 1)
-            if 0 <= i - 1:
-                quantise_kv(i - 1)
-            if i + 1 < WINDOWS:
-                quantise_x(i + 1)
-            if 0 <= i < WINDOWS:
-                project(i)
-            if 0 <= i - 1:
-                context(i - 1)
+        for half in range(HALVES):
+            transpose_x(0, half)
+        for half in range(HALVES):
+            quantise_x(0, half)
+
+        for w in range(WINDOWS):
+            kv_grouped[w] = twice.tile(
+                [P, HEADS, 2, HEAD_DIM, PACK], BF16, name="kv_grouped", align_bytes=64
+            )
+            kv_codes[w] = twice.tile([P, HEADS, 2, HEAD_DIM], U32, name="kv_codes", align_bytes=64)
+            kv_planes[w] = twice.tile([P, HEADS, 2, HEAD_DIM], U8, name="kv_planes", align_bytes=64)
+            for h in range(HEADS):
+                k = project(w, K, h)
+                v = project(w, V, h)
+                exp_k = four.tile([P, HEAD_DIM, PACK], F32, name="exp_k")
+                nc.scalar.activation(out=exp_k[:], in_=k, func=ACT.Exp)
+                nc.scalar.copy(out=kv_grouped[w][:, h, V, :, :], in_=v)
+                nc.vector.tensor_scalar(
+                    out=exp_k[:], in0=exp_k[:], scalar1=1.0, scalar2=None, op0=ALU.min
+                )
+                if h > 0:
+                    quantise_kv(w, h - 1)
+                elif w > 0:
+                    quantise_kv(w - 1, HEADS - 1)
+                nc.vector.scalar_tensor_tensor(
+                    out=kv_grouped[w][:, h, K, :, :],
+                    in0=k,
+                    scalar=0.0,
+                    in1=exp_k[:],
+                    op0=ALU.max,
+                    op1=ALU.add,
+                )
+                if h == 0:
+                    if w + 1 < WINDOWS:
+                        for half in range(HALVES):
+                            transpose_x(w + 1, half)
+                        quantise_x(w + 1, 0)
+                    if w > 0:
+                        context(w - 1)
+                    if w + 1 < WINDOWS:
+                        quantise_x(w + 1, 1)
+        quantise_kv(WINDOWS - 1, HEADS - 1)
+        context(WINDOWS - 1)

@@ -62,19 +62,25 @@ def tile_localcontextprocessor_pa_t_kernel(
 
         w_words = keep.tile([P, 2, GROUPS, INNER * PACK], U8, align_bytes=64)
 
-        load_x(0)
-        for kv, words in ((K, w_k_words), (V, w_v_words)):
+        def load_words(kv, words):
             nc.sync.dma_start(
                 out=w_words[:, kv, :, :].bitcast(I32),
                 in_=words.rearrange("g p n t -> p g (n t)").bitcast(I32),
             )
-        for kv, scales in ((K, w_k_scales), (V, w_v_scales)):
+
+        def load_scales(kv, scales):
             for quadrant in range(QUADRANTS):
                 rows = slice(4 * quadrant, 4 * quadrant + 4)
                 nc.sync.dma_start(
                     out=w_planes[32 * quadrant : 32 * quadrant + 4, kv, :, :].bitcast(I32),
                     in_=scales[:, rows, :].rearrange("g r n -> r g n").bitcast(I32),
                 )
+
+        load_x(0)
+        load_scales(K, w_k_scales)
+        load_words(K, w_k_words)
+        load_words(V, w_v_words)
+        load_scales(V, w_v_scales)
         for w in range(1, WINDOWS):
             load_x(w)
 

@@ -55,17 +55,20 @@ def tile_localcontextprocessor_pa_t_kernel(
             keep.tile([P, TOKEN_TILES, FEATURES], BF16, name="x_win%d" % w) for w in range(WINDOWS)
         ]
 
-        def load_x(w):
-            for half in range(HALVES):
-                tiles = slice(HALF_TILES * half, HALF_TILES * (half + 1))
+        def load_x(w, pieces):
+            first = 0
+            for piece in pieces:
+                tiles = slice(first, first + piece)
                 nc.sync.dma_start(out=x_tiles[w][:, tiles, :], in_=x_windows[w, :, tiles, :])
+                first += piece
 
         w_words = keep.tile([P, 2, GROUPS, INNER * PACK], U8, align_bytes=64)
 
-        def load_words(kv, words):
+        def load_words(kv, words, half):
+            cols = slice(INNER * PACK // 2 * half, INNER * PACK // 2 * (half + 1))
             nc.sync.dma_start(
-                out=w_words[:, kv, :, :].bitcast(I32),
-                in_=words.rearrange("g p n t -> p g (n t)").bitcast(I32),
+                out=w_words[:, kv, :, cols].bitcast(I32),
+                in_=words.rearrange("g p n t -> p g (n t)")[:, :, cols].bitcast(I32),
             )
 
         def load_scales(kv, scales):
@@ -76,64 +79,67 @@ def tile_localcontextprocessor_pa_t_kernel(
                     in_=scales[:, rows, :].rearrange("g r n -> r g n").bitcast(I32),
                 )
 
-        load_x(0)
+        load_x(0, (1, 1, 2))
         load_scales(K, w_k_scales)
-        load_words(K, w_k_words)
-        load_words(V, w_v_words)
+        load_words(K, w_k_words, 0)
         load_scales(V, w_v_scales)
+        load_words(V, w_v_words, 0)
+        load_words(K, w_k_words, 1)
+        load_words(V, w_v_words, 1)
         for w in range(1, WINDOWS):
-            load_x(w)
+            load_x(w, (2, 2))
 
         x_grouped, x_codes, x_planes = {}, {}, {}
         kv_grouped, kv_codes, kv_planes = {}, {}, {}
 
-        def transpose_x(w, half):
-            x_grouped[w, half] = four.tile(
-                [P, GROUPS, HALF, PACK], BF16, name="x_grouped", align_bytes=64
-            )
-            grouped_pairs = x_grouped[w, half][:].bitcast(F32)
+        def transpose_x(w, t):
             x_pairs = x_tiles[w][:].bitcast(F32)
             pairs_in_group = K_PASS // 2
+            flipped = banks.tile([P, GROUPS, PAIRS, P], F32, tag="bank")
             for g in range(GROUPS):
-                flipped = banks.tile([P, PAIRS, HALF], F32, tag="bank")
                 for u in range(PAIRS):
-                    for s in range(HALF_TILES):
-                        nc.tensor.transpose(
-                            flipped[:, u, P * s : P * (s + 1)],
-                            x_pairs[
-                                :,
-                                HALF_TILES * half + s,
-                                pairs_in_group * g + u : pairs_in_group * (g + 1) : PAIRS,
-                            ],
-                            identity[:],
-                        )
-                nc.scalar.copy(
-                    out=grouped_pairs[:, g, :, :], in_=flipped[:].rearrange("p u n -> p n u")
+                    nc.tensor.transpose(
+                        flipped[:, g, u, :],
+                        x_pairs[:, t, pairs_in_group * g + u : pairs_in_group * (g + 1) : PAIRS],
+                        identity[:],
+                    )
+            return flipped
+
+        def group_x(w, t, flipped, copy):
+            half = t // HALF_TILES
+            if t % HALF_TILES == 0:
+                x_grouped[w, half] = four.tile(
+                    [P, HALF_TILES, GROUPS, P, PACK], BF16, name="x_grouped", align_bytes=64
                 )
+            grouped_pairs = x_grouped[w, half][:].bitcast(F32)
+            copy(
+                out=grouped_pairs[:, t % HALF_TILES, :, :, :],
+                in_=flipped[:].rearrange("p g u n -> p g n u"),
+            )
 
         def quantise_x(w, half):
             if half == 0:
                 x_codes[w] = twice.tile(
-                    [P, HALVES, GROUPS, HALF], U32, name="x_codes", align_bytes=64
+                    [P, TOKEN_TILES, GROUPS, P], U32, name="x_codes", align_bytes=64
                 )
                 x_planes[w] = twice.tile(
-                    [P, HALVES, GROUPS, HALF], U8, name="x_planes", align_bytes=64
+                    [P, TOKEN_TILES, GROUPS, P], U8, name="x_planes", align_bytes=64
                 )
+            tiles = slice(HALF_TILES * half, HALF_TILES * (half + 1))
             nc.vector.quantize_mx(
-                out=x_codes[w][:, half, :, :].rearrange("p g n -> p (g n)").bitcast(FP8X4),
-                scales=x_planes[w][:, half, :, :].rearrange("p g n -> p (g n)"),
-                in_=x_grouped[w, half][:].rearrange("p g n k -> p (g n k)"),
+                out=x_codes[w][:, tiles, :, :].rearrange("p t g n -> p (t g n)").bitcast(FP8X4),
+                scales=x_planes[w][:, tiles, :, :].rearrange("p t g n -> p (t g n)"),
+                in_=x_grouped[w, half][:].rearrange("p t g n k -> p (t g n k)"),
             )
 
         def project(w, kv, h):
             product = banks.tile([P, TOKEN_TILES, HEAD_DIM], F32, tag="bank")
             for t in range(TOKEN_TILES):
-                half, tokens = t // HALF_TILES, slice(P * (t % HALF_TILES), P * (t % HALF_TILES + 1))
                 for g in range(GROUPS):
                     nc.tensor.matmul_mx(
                         out=product[:, t, :],
-                        lhsT=x_codes[w][:, half, g, tokens].bitcast(FP8X4),
-                        lhsT_scale=x_planes[w][:, half, g, tokens],
+                        lhsT=x_codes[w][:, t, g, :].bitcast(FP8X4),
+                        lhsT_scale=x_planes[w][:, t, g, :],
                         rhs=w_words[
                             :, kv, g, PACK * HEAD_DIM * h : PACK * HEAD_DIM * (h + 1)
                         ].bitcast(FP8X4),
@@ -150,11 +156,11 @@ def tile_localcontextprocessor_pa_t_kernel(
                 in_=kv_grouped[w][:, h, :, :, :].rearrange("p s c t -> p (s c t)"),
             )
 
-        def context(w):
-            product = banks.tile([P, HEADS, HEAD_DIM], F32, tag="bank")
-            for h in range(HEADS):
+        def context(w, heads, copy):
+            product = banks.tile([P, len(heads), HEAD_DIM], F32, tag="bank")
+            for i, h in enumerate(heads):
                 nc.tensor.matmul_mx(
-                    out=product[:, h, :],
+                    out=product[:, i, :],
                     lhsT=kv_codes[w][:, h, K, :].bitcast(FP8X4),
                     lhsT_scale=kv_planes[w][:, h, K, :],
                     rhs=kv_codes[w][:, h, V, :].bitcast(FP8X4),
@@ -162,12 +168,14 @@ def tile_localcontextprocessor_pa_t_kernel(
                     start=True,
                     stop=True,
                 )
-            result = twice.tile([P, HEADS, HEAD_DIM], F32, name="result")
-            nc.vector.tensor_copy(out=result[:], in_=product[:])
-            nc.sync.dma_start(out=out[w].rearrange("h d e -> d h e"), in_=result[:])
+            result = four.tile([P, len(heads), HEAD_DIM], F32, name="result")
+            copy(out=result[:], in_=product[:])
+            nc.sync.dma_start(
+                out=out[w, heads[0] : heads[-1] + 1].rearrange("h d e -> d h e"), in_=result[:]
+            )
 
-        for half in range(HALVES):
-            transpose_x(0, half)
+        for t in range(TOKEN_TILES):
+            group_x(0, t, transpose_x(0, t), nc.vector.tensor_copy if t % 2 else nc.scalar.copy)
         for half in range(HALVES):
             quantise_x(0, half)
 
@@ -177,6 +185,7 @@ def tile_localcontextprocessor_pa_t_kernel(
             )
             kv_codes[w] = twice.tile([P, HEADS, 2, HEAD_DIM], U32, name="kv_codes", align_bytes=64)
             kv_planes[w] = twice.tile([P, HEADS, 2, HEAD_DIM], U8, name="kv_planes", align_bytes=64)
+            transposing_head = 1 if w == 0 else 0
             for h in range(HEADS):
                 k = project(w, K, h)
                 v = project(w, V, h)
@@ -198,14 +207,15 @@ def tile_localcontextprocessor_pa_t_kernel(
                     op0=ALU.max,
                     op1=ALU.add,
                 )
-                if h == 0:
+                if h == transposing_head:
                     if w + 1 < WINDOWS:
-                        for half in range(HALVES):
-                            transpose_x(w + 1, half)
+                        for t in range(TOKEN_TILES):
+                            group_x(w + 1, t, transpose_x(w + 1, t), nc.scalar.copy)
                         quantise_x(w + 1, 0)
                     if w > 0:
-                        context(w - 1)
+                        context(w - 1, range(HEADS), nc.vector.tensor_copy)
                     if w + 1 < WINDOWS:
                         quantise_x(w + 1, 1)
+        context(WINDOWS - 1, range(HEADS - 1), nc.scalar.copy)
         quantise_kv(WINDOWS - 1, HEADS - 1)
-        context(WINDOWS - 1)
+        context(WINDOWS - 1, range(HEADS - 1, HEADS), nc.vector.tensor_copy)

@@ -79,7 +79,7 @@ def tile_localcontextprocessor_pa_t_kernel(
                     in_=scales[:, rows, :].rearrange("g r n -> r g n").bitcast(I32),
                 )
 
-        load_x(0, (1, 1, 2))
+        load_x(0, (1, 1, 1, 1))
         load_scales(K, w_k_scales)
         load_words(K, w_k_words, 0)
         load_scales(V, w_v_scales)
@@ -92,44 +92,46 @@ def tile_localcontextprocessor_pa_t_kernel(
         x_grouped, x_codes, x_planes = {}, {}, {}
         kv_grouped, kv_codes, kv_planes = {}, {}, {}
 
-        def transpose_x(w, t):
+        def transpose_x(w, t, groups):
             x_pairs = x_tiles[w][:].bitcast(F32)
             pairs_in_group = K_PASS // 2
-            flipped = banks.tile([P, GROUPS, PAIRS, P], F32, tag="bank")
-            for g in range(GROUPS):
+            flipped = banks.tile([P, len(groups), PAIRS, P], F32, tag="bank")
+            for i, g in enumerate(groups):
                 for u in range(PAIRS):
                     nc.tensor.transpose(
-                        flipped[:, g, u, :],
+                        flipped[:, i, u, :],
                         x_pairs[:, t, pairs_in_group * g + u : pairs_in_group * (g + 1) : PAIRS],
                         identity[:],
                     )
             return flipped
 
-        def group_x(w, t, flipped, copy):
+        def group_x(w, t, groups, flipped, copy):
             half = t // HALF_TILES
-            if t % HALF_TILES == 0:
+            if (w, half) not in x_grouped:
                 x_grouped[w, half] = four.tile(
                     [P, HALF_TILES, GROUPS, P, PACK], BF16, name="x_grouped", align_bytes=64
                 )
             grouped_pairs = x_grouped[w, half][:].bitcast(F32)
             copy(
-                out=grouped_pairs[:, t % HALF_TILES, :, :, :],
+                out=grouped_pairs[:, t % HALF_TILES, groups[0] : groups[-1] + 1, :, :],
                 in_=flipped[:].rearrange("p g u n -> p g n u"),
             )
 
-        def quantise_x(w, half):
-            if half == 0:
+        def quantise_x(w, tiles):
+            if w not in x_codes:
                 x_codes[w] = twice.tile(
                     [P, TOKEN_TILES, GROUPS, P], U32, name="x_codes", align_bytes=64
                 )
                 x_planes[w] = twice.tile(
                     [P, TOKEN_TILES, GROUPS, P], U8, name="x_planes", align_bytes=64
                 )
-            tiles = slice(HALF_TILES * half, HALF_TILES * (half + 1))
+            cut = slice(tiles[0], tiles[-1] + 1)
+            cut_in_half = slice(tiles[0] % HALF_TILES, tiles[-1] % HALF_TILES + 1)
+            grouped = x_grouped[w, tiles[0] // HALF_TILES]
             nc.vector.quantize_mx(
-                out=x_codes[w][:, tiles, :, :].rearrange("p t g n -> p (t g n)").bitcast(FP8X4),
-                scales=x_planes[w][:, tiles, :, :].rearrange("p t g n -> p (t g n)"),
-                in_=x_grouped[w, half][:].rearrange("p t g n k -> p (t g n k)"),
+                out=x_codes[w][:, cut, :, :].rearrange("p t g n -> p (t g n)").bitcast(FP8X4),
+                scales=x_planes[w][:, cut, :, :].rearrange("p t g n -> p (t g n)"),
+                in_=grouped[:, cut_in_half, :, :, :].rearrange("p t g n k -> p (t g n k)"),
             )
 
         def project(w, kv, h):
@@ -175,9 +177,11 @@ def tile_localcontextprocessor_pa_t_kernel(
             )
 
         for t in range(TOKEN_TILES):
-            group_x(0, t, transpose_x(0, t), nc.vector.tensor_copy if t % 2 else nc.scalar.copy)
-        for half in range(HALVES):
-            quantise_x(0, half)
+            group_x(0, t, range(0, 1), transpose_x(0, t, range(0, 1)), nc.scalar.copy)
+            group_x(0, t, range(1, 2), transpose_x(0, t, range(1, 2)), nc.vector.tensor_copy)
+            if t > 0:
+                quantise_x(0, range(t - 1, t))
+        quantise_x(0, range(TOKEN_TILES - 1, TOKEN_TILES))
 
         for w in range(WINDOWS):
             kv_grouped[w] = twice.tile(
@@ -185,7 +189,7 @@ def tile_localcontextprocessor_pa_t_kernel(
             )
             kv_codes[w] = twice.tile([P, HEADS, 2, HEAD_DIM], U32, name="kv_codes", align_bytes=64)
             kv_planes[w] = twice.tile([P, HEADS, 2, HEAD_DIM], U8, name="kv_planes", align_bytes=64)
-            transposing_head = 1 if w == 0 else 0
+            transposing_head = 1 if w in (0, WINDOWS - 1) else 0
             for h in range(HEADS):
                 k = project(w, K, h)
                 v = project(w, V, h)
@@ -210,12 +214,18 @@ def tile_localcontextprocessor_pa_t_kernel(
                 if h == transposing_head:
                     if w + 1 < WINDOWS:
                         for t in range(TOKEN_TILES):
-                            group_x(w + 1, t, transpose_x(w + 1, t), nc.scalar.copy)
-                        quantise_x(w + 1, 0)
+                            group_x(
+                                w + 1,
+                                t,
+                                range(GROUPS),
+                                transpose_x(w + 1, t, range(GROUPS)),
+                                nc.scalar.copy,
+                            )
+                        quantise_x(w + 1, range(HALF_TILES))
                     if w > 0:
                         context(w - 1, range(HEADS), nc.vector.tensor_copy)
                     if w + 1 < WINDOWS:
-                        quantise_x(w + 1, 1)
+                        quantise_x(w + 1, range(HALF_TILES, TOKEN_TILES))
         context(WINDOWS - 1, range(HEADS - 1), nc.scalar.copy)
         quantise_kv(WINDOWS - 1, HEADS - 1)
         context(WINDOWS - 1, range(HEADS - 1, HEADS), nc.vector.tensor_copy)

@@ -27,6 +27,7 @@ HALVES = 2
 HALF_TILES = TOKEN_TILES // HALVES
 HALF = HALF_TILES * P
 PAIRS = 2
+TURNED_TILES = 3
 QUADRANTS = 4
 K, V = 0, 1
 
@@ -89,8 +90,21 @@ def tile_localcontextprocessor_pa_t_kernel(
         for w in range(1, WINDOWS):
             load_x(w, (2, 2))
 
-        x_grouped, x_codes, x_planes = {}, {}, {}
+        x_turned, x_grouped, x_codes, x_planes = {}, {}, {}, {}
         kv_grouped, kv_codes, kv_planes = {}, {}, {}
+
+        def turn_x(w, tiles):
+            if w not in x_turned:
+                x_turned[w] = twice.tile(
+                    [P, TURNED_TILES, GROUPS, PAIRS, P], F32, name="x_turned", align_bytes=64
+                )
+            cut = slice(tiles[0], tiles[-1] + 1)
+            nc.vector.tensor_copy(
+                out=x_turned[w][:, cut, :, :, :],
+                in_=x_tiles[w][:, cut, :]
+                .bitcast(F32)
+                .rearrange("p t (g n u) -> p t g u n", g=GROUPS, u=PAIRS),
+            )
 
         def transpose_x(w, t, groups):
             x_pairs = x_tiles[w][:].bitcast(F32)
@@ -98,11 +112,13 @@ def tile_localcontextprocessor_pa_t_kernel(
             flipped = banks.tile([P, len(groups), PAIRS, P], F32, tag="bank")
             for i, g in enumerate(groups):
                 for u in range(PAIRS):
-                    nc.tensor.transpose(
-                        flipped[:, i, u, :],
-                        x_pairs[:, t, pairs_in_group * g + u : pairs_in_group * (g + 1) : PAIRS],
-                        identity[:],
-                    )
+                    if w in x_turned and t < TURNED_TILES:
+                        words = x_turned[w][:, t, g, u, :]
+                    else:
+                        words = x_pairs[
+                            :, t, pairs_in_group * g + u : pairs_in_group * (g + 1) : PAIRS
+                        ]
+                    nc.tensor.transpose(flipped[:, i, u, :], words, identity[:])
             return flipped
 
         def group_x(w, t, groups, flipped, copy):
@@ -221,9 +237,13 @@ def tile_localcontextprocessor_pa_t_kernel(
                                 transpose_x(w + 1, t, range(GROUPS)),
                                 nc.scalar.copy,
                             )
+                        if w + 2 < WINDOWS:
+                            turn_x(w + 2, range(HALF_TILES))
                         quantise_x(w + 1, range(HALF_TILES))
                     if w > 0:
                         context(w - 1, range(HEADS), nc.vector.tensor_copy)
+                    if w + 2 < WINDOWS:
+                        turn_x(w + 2, range(HALF_TILES, TURNED_TILES))
                     if w + 1 < WINDOWS:
                         quantise_x(w + 1, range(HALF_TILES, TOKEN_TILES))
         context(WINDOWS - 1, range(HEADS - 1), nc.scalar.copy)

@@ -241,7 +241,7 @@ def tile_localcontextprocessor_pa_t_kernel(
                             turn_x(w + 2, range(HALF_TILES))
                         quantise_x(w + 1, range(HALF_TILES))
                     if w > 0:
-                        context(w - 1, range(HEADS), nc.vector.tensor_copy)
+                        context(w - 1, range(HEADS), nc.scalar.copy)
                     if w + 2 < WINDOWS:
                         turn_x(w + 2, range(HALF_TILES, TURNED_TILES))
                     if w + 1 < WINDOWS:

@@ -29,6 +29,8 @@ HALF = HALF_TILES * P
 PAIRS = 2
 TURNED_TILES = 3
 QUADRANTS = 4
+WHOLE_RUN = (range(TOKEN_TILES),)
+HALF_RUNS = (range(HALF_TILES), range(HALF_TILES, TOKEN_TILES))
 K, V = 0, 1
 
 FLOPS = 2 * BATCH * TOKENS * FEATURES * 2 * INNER + 2 * WINDOWS * HEADS * WINDOW * HEAD_DIM * HEAD_DIM
@@ -150,22 +152,29 @@ def tile_localcontextprocessor_pa_t_kernel(
                 in_=grouped[:, cut_in_half, :, :, :].rearrange("p t g n k -> p (t g n k)"),
             )
 
-        def project(w, kv, h):
-            product = banks.tile([P, TOKEN_TILES, HEAD_DIM], F32, tag="bank")
-            for t in range(TOKEN_TILES):
-                for g in range(GROUPS):
-                    nc.tensor.matmul_mx(
-                        out=product[:, t, :],
-                        lhsT=x_codes[w][:, t, g, :].bitcast(FP8X4),
-                        lhsT_scale=x_planes[w][:, t, g, :],
-                        rhs=w_words[
-                            :, kv, g, PACK * HEAD_DIM * h : PACK * HEAD_DIM * (h + 1)
-                        ].bitcast(FP8X4),
-                        rhs_scale=w_planes[:, kv, g, HEAD_DIM * h : HEAD_DIM * (h + 1)],
-                        start=(g == 0),
-                        stop=(g == GROUPS - 1),
-                    )
-            return product[:].rearrange("p t c -> p c t")
+        def project(w, heads, tile_runs):
+            wanted = [(kv, h) for h in heads for kv in (K, V)]
+            products = {}
+            for tiles in tile_runs:
+                for kv, h in wanted:
+                    if (kv, h) not in products:
+                        products[kv, h] = banks.tile(
+                            [P, TOKEN_TILES, HEAD_DIM], F32, name="product", tag="bank"
+                        )
+                    for t in tiles:
+                        for g in range(GROUPS):
+                            nc.tensor.matmul_mx(
+                                out=products[kv, h][:, t, :],
+                                lhsT=x_codes[w][:, t, g, :].bitcast(FP8X4),
+                                lhsT_scale=x_planes[w][:, t, g, :],
+                                rhs=w_words[
+                                    :, kv, g, PACK * HEAD_DIM * h : PACK * HEAD_DIM * (h + 1)
+                                ].bitcast(FP8X4),
+                                rhs_scale=w_planes[:, kv, g, HEAD_DIM * h : HEAD_DIM * (h + 1)],
+                                start=(g == 0),
+                                stop=(g == GROUPS - 1),
+                            )
+            return {key: products[key][:].rearrange("p t c -> p c t") for key in wanted}
 
         def quantise_kv(w, h):
             nc.vector.quantize_mx(
@@ -205,11 +214,14 @@ def tile_localcontextprocessor_pa_t_kernel(
             )
             kv_codes[w] = twice.tile([P, HEADS, 2, HEAD_DIM], U32, name="kv_codes", align_bytes=64)
             kv_planes[w] = twice.tile([P, HEADS, 2, HEAD_DIM], U8, name="kv_planes", align_bytes=64)
-            transposing_head = 1 if w in (0, WINDOWS - 1) else 0
+            transposing_head = 1 if w == 0 else 0
             for h in range(HEADS):
-                k = project(w, K, h)
-                v = project(w, V, h)
-                exp_k = four.tile([P, HEAD_DIM, PACK], F32, name="exp_k")
+                if w == 0 and h == 0:
+                    kv_psum = project(w, range(2), HALF_RUNS)
+                elif w > 0 or h > 1:
+                    kv_psum = project(w, range(h, h + 1), WHOLE_RUN)
+                k, v = kv_psum[K, h], kv_psum[V, h]
+                exp_k = four.tile([P, HEAD_DIM, PACK], BF16, name="exp_k")
                 nc.scalar.activation(out=exp_k[:], in_=k, func=ACT.Exp)
                 nc.scalar.copy(out=kv_grouped[w][:, h, V, :, :], in_=v)
                 nc.vector.tensor_scalar(
@@ -240,12 +252,12 @@ def tile_localcontextprocessor_pa_t_kernel(
                         if w + 2 < WINDOWS:
                             turn_x(w + 2, range(HALF_TILES))
                         quantise_x(w + 1, range(HALF_TILES))
-                    if w > 0:
-                        context(w - 1, range(HEADS), nc.scalar.copy)
                     if w + 2 < WINDOWS:
                         turn_x(w + 2, range(HALF_TILES, TURNED_TILES))
                     if w + 1 < WINDOWS:
                         quantise_x(w + 1, range(HALF_TILES, TOKEN_TILES))
+                if h == 1 and w > 0:
+                    context(w - 1, range(HEADS), nc.vector.tensor_copy if w % 2 else nc.scalar.copy)
         context(WINDOWS - 1, range(HEADS - 1), nc.scalar.copy)
         quantise_kv(WINDOWS - 1, HEADS - 1)
         context(WINDOWS - 1, range(HEADS - 1, HEADS), nc.vector.tensor_copy)

@@ -31,6 +31,7 @@ TURNED_TILES = 3
 QUADRANTS = 4
 WHOLE_RUN = (range(TOKEN_TILES),)
 HALF_RUNS = (range(HALF_TILES), range(HALF_TILES, TOKEN_TILES))
+WARM_COLS = 512
 K, V = 0, 1
 
 FLOPS = 2 * BATCH * TOKENS * FEATURES * 2 * INNER + 2 * WINDOWS * HEADS * WINDOW * HEAD_DIM * HEAD_DIM
@@ -49,6 +50,8 @@ def tile_localcontextprocessor_pa_t_kernel(
         four = ctx.enter_context(tc.tile_pool(name="four", bufs=4))
         banks = ctx.enter_context(tc.psum_pool(name="banks", bufs=8))
 
+        warm = keep.tile([P, WARM_COLS], BF16)
+        nc.vector.memset(warm[:], 0.0)
         w_planes = keep.tile([P, 2, GROUPS, INNER], U8, align_bytes=64)
         nc.vector.memset(w_planes[:].bitcast(I32), 0)
         identity = keep.tile([P, P], F32)
@@ -108,10 +111,18 @@ def tile_localcontextprocessor_pa_t_kernel(
                 .rearrange("p t (g n u) -> p t g u n", g=GROUPS, u=PAIRS),
             )
 
-        def transpose_x(w, t, groups):
+        def transpose_x(w, t, groups, busy=False):
             x_pairs = x_tiles[w][:].bitcast(F32)
             pairs_in_group = K_PASS // 2
             flipped = banks.tile([P, len(groups), PAIRS, P], F32, tag="bank")
+            if busy:
+                nc.tensor.matmul(
+                    flipped[:].rearrange("p g u n -> p (g u n)"),
+                    lhsT=warm[:, :P],
+                    rhs=warm[:, : len(groups) * PAIRS * P],
+                    start=True,
+                    stop=True,
+                )
             for i, g in enumerate(groups):
                 for u in range(PAIRS):
                     if w in x_turned and t < TURNED_TILES:
@@ -152,8 +163,7 @@ def tile_localcontextprocessor_pa_t_kernel(
                 in_=grouped[:, cut_in_half, :, :, :].rearrange("p t g n k -> p (t g n k)"),
             )
 
-        def project(w, heads, tile_runs):
-            wanted = [(kv, h) for h in heads for kv in (K, V)]
+        def project(w, wanted, tile_runs):
             products = {}
             for tiles in tile_runs:
                 for kv, h in wanted:
@@ -176,11 +186,12 @@ def tile_localcontextprocessor_pa_t_kernel(
                             )
             return {key: products[key][:].rearrange("p t c -> p c t") for key in wanted}
 
-        def quantise_kv(w, h):
+        def quantise_kv(w, h, first=K, last=V):
+            cut = slice(first, last + 1)
             nc.vector.quantize_mx(
-                out=kv_codes[w][:, h, :, :].rearrange("p s c -> p (s c)").bitcast(FP8X4),
-                scales=kv_planes[w][:, h, :, :].rearrange("p s c -> p (s c)"),
-                in_=kv_grouped[w][:, h, :, :, :].rearrange("p s c t -> p (s c t)"),
+                out=kv_codes[w][:, h, cut, :].rearrange("p s c -> p (s c)").bitcast(FP8X4),
+                scales=kv_planes[w][:, h, cut, :].rearrange("p s c -> p (s c)"),
+                in_=kv_grouped[w][:, h, cut, :, :].rearrange("p s c t -> p (s c t)"),
             )
 
         def context(w, heads, copy):
@@ -201,12 +212,38 @@ def tile_localcontextprocessor_pa_t_kernel(
                 out=out[w, heads[0] : heads[-1] + 1].rearrange("h d e -> d h e"), in_=result[:]
             )
 
+        idle = banks.tile([P, WARM_COLS], F32, name="idle", tag="bank")
+        for repeat in range(5):
+            nc.tensor.matmul(idle[:], lhsT=warm[:, :P], rhs=warm[:], start=True, stop=True)
         for t in range(TOKEN_TILES):
-            group_x(0, t, range(0, 1), transpose_x(0, t, range(0, 1)), nc.scalar.copy)
+            group_x(0, t, range(0, 1), transpose_x(0, t, range(0, 1), t == 2), nc.scalar.copy)
             group_x(0, t, range(1, 2), transpose_x(0, t, range(1, 2)), nc.vector.tensor_copy)
             if t > 0:
                 quantise_x(0, range(t - 1, t))
         quantise_x(0, range(TOKEN_TILES - 1, TOKEN_TILES))
+
+        def exponential(k):
+            exp_k = four.tile([P, HEAD_DIM, PACK], BF16, name="exp_k")
+            nc.scalar.activation(out=exp_k[:], in_=k, func=ACT.Exp)
+            return exp_k
+
+        def clip(exp_k):
+            nc.vector.tensor_scalar(
+                out=exp_k[:], in0=exp_k[:], scalar1=1.0, scalar2=None, op0=ALU.min
+            )
+
+        def finish_kf(w, h, k, exp_k):
+            nc.vector.scalar_tensor_tensor(
+                out=kv_grouped[w][:, h, K, :, :],
+                in0=k,
+                scalar=0.0,
+                in1=exp_k[:],
+                op0=ALU.max,
+                op1=ALU.add,
+            )
+
+        def group_v(w, h, v):
+            nc.scalar.copy(out=kv_grouped[w][:, h, V, :, :], in_=v)
 
         for w in range(WINDOWS):
             kv_grouped[w] = twice.tile(
@@ -214,50 +251,55 @@ def tile_localcontextprocessor_pa_t_kernel(
             )
             kv_codes[w] = twice.tile([P, HEADS, 2, HEAD_DIM], U32, name="kv_codes", align_bytes=64)
             kv_planes[w] = twice.tile([P, HEADS, 2, HEAD_DIM], U8, name="kv_planes", align_bytes=64)
+            if w == WINDOWS - 1:
+                break
             transposing_head = 1 if w == 0 else 0
             for h in range(HEADS):
                 if w == 0 and h == 0:
-                    kv_psum = project(w, range(2), HALF_RUNS)
+                    kv_psum = project(w, ((K, 0), (V, 0), (K, 1), (V, 1)), HALF_RUNS)
                 elif w > 0 or h > 1:
-                    kv_psum = project(w, range(h, h + 1), WHOLE_RUN)
-                k, v = kv_psum[K, h], kv_psum[V, h]
-                exp_k = four.tile([P, HEAD_DIM, PACK], BF16, name="exp_k")
-                nc.scalar.activation(out=exp_k[:], in_=k, func=ACT.Exp)
-                nc.scalar.copy(out=kv_grouped[w][:, h, V, :, :], in_=v)
-                nc.vector.tensor_scalar(
-                    out=exp_k[:], in0=exp_k[:], scalar1=1.0, scalar2=None, op0=ALU.min
-                )
+                    kv_psum = project(w, ((K, h), (V, h)), WHOLE_RUN)
+                exp_k = exponential(kv_psum[K, h])
+                group_v(w, h, kv_psum[V, h])
+                clip(exp_k)
                 if h > 0:
                     quantise_kv(w, h - 1)
                 elif w > 0:
                     quantise_kv(w - 1, HEADS - 1)
-                nc.vector.scalar_tensor_tensor(
-                    out=kv_grouped[w][:, h, K, :, :],
-                    in0=k,
-                    scalar=0.0,
-                    in1=exp_k[:],
-                    op0=ALU.max,
-                    op1=ALU.add,
-                )
+                finish_kf(w, h, kv_psum[K, h], exp_k)
                 if h == transposing_head:
-                    if w + 1 < WINDOWS:
-                        for t in range(TOKEN_TILES):
-                            group_x(
-                                w + 1,
-                                t,
-                                range(GROUPS),
-                                transpose_x(w + 1, t, range(GROUPS)),
-                                nc.scalar.copy,
-                            )
-                        if w + 2 < WINDOWS:
-                            turn_x(w + 2, range(HALF_TILES))
-                        quantise_x(w + 1, range(HALF_TILES))
+                    for t in range(TOKEN_TILES):
+                        group_x(
+                            w + 1,
+                            t,
+                            range(GROUPS),
+                            transpose_x(w + 1, t, range(GROUPS)),
+                            nc.scalar.copy,
+                        )
+                    if w + 2 < WINDOWS:
+                        turn_x(w + 2, range(HALF_TILES))
+                    quantise_x(w + 1, range(HALF_TILES))
                     if w + 2 < WINDOWS:
                         turn_x(w + 2, range(HALF_TILES, TURNED_TILES))
-                    if w + 1 < WINDOWS:
-                        quantise_x(w + 1, range(HALF_TILES, TOKEN_TILES))
-                if h == 1 and w > 0:
+                    quantise_x(w + 1, range(HALF_TILES, TOKEN_TILES))
+                if h == 2 and w > 0:
                     context(w - 1, range(HEADS), nc.vector.tensor_copy if w % 2 else nc.scalar.copy)
-        context(WINDOWS - 1, range(HEADS - 1), nc.scalar.copy)
-        quantise_kv(WINDOWS - 1, HEADS - 1)
-        context(WINDOWS - 1, range(HEADS - 1, HEADS), nc.vector.tensor_copy)
+
+        w = WINDOWS - 1
+        for h in range(HEADS):
+            k = project(w, ((K, h),), WHOLE_RUN)[K, h]
+            exp_k = exponential(k)
+            clip(exp_k)
+            if h == 0:
+                quantise_kv(w - 1, HEADS - 1)
+            elif h > 1:
+                quantise_kv(w, h - 2, K, K)
+            finish_kf(w, h, k, exp_k)
+        context(w - 1, range(HEADS), nc.scalar.copy)
+        for h in (HEADS - 2, HEADS - 1):
+            quantise_kv(w, h, K, K)
+        for h in range(HEADS):
+            group_v(w, h, project(w, ((V, h),), WHOLE_RUN)[V, h])
+            quantise_kv(w, h, V, V)
+        context(w, range(HEADS - 1), nc.vector.tensor_copy)
+        context(w, range(HEADS - 1, HEADS), nc.scalar.copy)

@@ -31,7 +31,6 @@ TURNED_TILES = 3
 QUADRANTS = 4
 WHOLE_RUN = (range(TOKEN_TILES),)
 HALF_RUNS = (range(HALF_TILES), range(HALF_TILES, TOKEN_TILES))
-WARM_COLS = 512
 K, V = 0, 1
 
 FLOPS = 2 * BATCH * TOKENS * FEATURES * 2 * INNER + 2 * WINDOWS * HEADS * WINDOW * HEAD_DIM * HEAD_DIM
@@ -50,8 +49,6 @@ def tile_localcontextprocessor_pa_t_kernel(
         four = ctx.enter_context(tc.tile_pool(name="four", bufs=4))
         banks = ctx.enter_context(tc.psum_pool(name="banks", bufs=8))
 
-        warm = keep.tile([P, WARM_COLS], BF16)
-        nc.vector.memset(warm[:], 0.0)
         w_planes = keep.tile([P, 2, GROUPS, INNER], U8, align_bytes=64)
         nc.vector.memset(w_planes[:].bitcast(I32), 0)
         identity = keep.tile([P, P], F32)
@@ -61,8 +58,7 @@ def tile_localcontextprocessor_pa_t_kernel(
             keep.tile([P, TOKEN_TILES, FEATURES], BF16, name="x_win%d" % w) for w in range(WINDOWS)
         ]
 
-        def load_x(w, pieces):
-            first = 0
+        def load_x(w, first, pieces):
             for piece in pieces:
                 tiles = slice(first, first + piece)
                 nc.sync.dma_start(out=x_tiles[w][:, tiles, :], in_=x_windows[w, :, tiles, :])
@@ -85,15 +81,17 @@ def tile_localcontextprocessor_pa_t_kernel(
                     in_=scales[:, rows, :].rearrange("g r n -> r g n").bitcast(I32),
                 )
 
-        load_x(0, (1, 1, 1, 1))
+        load_x(0, 0, (1,))
         load_scales(K, w_k_scales)
-        load_words(K, w_k_words, 0)
+        load_x(0, 1, (1, 1, 1))
         load_scales(V, w_v_scales)
+        load_words(K, w_k_words, 0)
         load_words(V, w_v_words, 0)
+        load_x(1, 0, (2, 2))
         load_words(K, w_k_words, 1)
         load_words(V, w_v_words, 1)
-        for w in range(1, WINDOWS):
-            load_x(w, (2, 2))
+        for w in range(2, WINDOWS):
+            load_x(w, 0, (2, 2))
 
         x_turned, x_grouped, x_codes, x_planes = {}, {}, {}, {}
         kv_grouped, kv_codes, kv_planes = {}, {}, {}
@@ -111,18 +109,10 @@ def tile_localcontextprocessor_pa_t_kernel(
                 .rearrange("p t (g n u) -> p t g u n", g=GROUPS, u=PAIRS),
             )
 
-        def transpose_x(w, t, groups, busy=False):
+        def transpose_x(w, t, groups):
             x_pairs = x_tiles[w][:].bitcast(F32)
             pairs_in_group = K_PASS // 2
             flipped = banks.tile([P, len(groups), PAIRS, P], F32, tag="bank")
-            if busy:
-                nc.tensor.matmul(
-                    flipped[:].rearrange("p g u n -> p (g u n)"),
-                    lhsT=warm[:, :P],
-                    rhs=warm[:, : len(groups) * PAIRS * P],
-                    start=True,
-                    stop=True,
-                )
             for i, g in enumerate(groups):
                 for u in range(PAIRS):
                     if w in x_turned and t < TURNED_TILES:
@@ -212,12 +202,10 @@ def tile_localcontextprocessor_pa_t_kernel(
                 out=out[w, heads[0] : heads[-1] + 1].rearrange("h d e -> d h e"), in_=result[:]
             )
 
-        idle = banks.tile([P, WARM_COLS], F32, name="idle", tag="bank")
-        for repeat in range(5):
-            nc.tensor.matmul(idle[:], lhsT=warm[:, :P], rhs=warm[:], start=True, stop=True)
         for t in range(TOKEN_TILES):
-            group_x(0, t, range(0, 1), transpose_x(0, t, range(0, 1), t == 2), nc.scalar.copy)
-            group_x(0, t, range(1, 2), transpose_x(0, t, range(1, 2)), nc.vector.tensor_copy)
+            group_x(0, t, range(0, 1), transpose_x(0, t, range(0, 1)), nc.scalar.copy)
+            copy = nc.vector.tensor_copy if t == 0 else nc.scalar.copy
+            group_x(0, t, range(1, 2), transpose_x(0, t, range(1, 2)), copy)
             if t > 0:
                 quantise_x(0, range(t - 1, t))
         quantise_x(0, range(TOKEN_TILES - 1, TOKEN_TILES))
@@ -256,17 +244,21 @@ def tile_localcontextprocessor_pa_t_kernel(
             transposing_head = 1 if w == 0 else 0
             for h in range(HEADS):
                 if w == 0 and h == 0:
-                    kv_psum = project(w, ((K, 0), (V, 0), (K, 1), (V, 1)), HALF_RUNS)
+                    k_psum = project(w, ((K, 0), (K, 1)), HALF_RUNS)
+                    v_psum = project(w, ((V, 0), (V, 1)), WHOLE_RUN)
+                    exps = [exponential(k_psum[K, 0]), exponential(k_psum[K, 1])]
                 elif w > 0 or h > 1:
-                    kv_psum = project(w, ((K, h), (V, h)), WHOLE_RUN)
-                exp_k = exponential(kv_psum[K, h])
-                group_v(w, h, kv_psum[V, h])
+                    k_psum = project(w, ((K, h),), WHOLE_RUN)
+                    v_psum = project(w, ((V, h),), WHOLE_RUN)
+                    exps = [exponential(k_psum[K, h])]
+                exp_k = exps[h if w == 0 and h < 2 else 0]
+                group_v(w, h, v_psum[V, h])
                 clip(exp_k)
                 if h > 0:
                     quantise_kv(w, h - 1)
                 elif w > 0:
                     quantise_kv(w - 1, HEADS - 1)
-                finish_kf(w, h, kv_psum[K, h], exp_k)
+                finish_kf(w, h, k_psum[K, h], exp_k)
                 if h == transposing_head:
                     for t in range(TOKEN_TILES):
                         group_x(

@@ -29,6 +29,7 @@ HALF = HALF_TILES * P
 PAIRS = 2
 TURNED_TILES = 3
 QUADRANTS = 4
+SHIFT = 32
 WHOLE_RUN = (range(TOKEN_TILES),)
 HALF_RUNS = (range(HALF_TILES), range(HALF_TILES, TOKEN_TILES))
 K, V = 0, 1
@@ -64,7 +65,7 @@ def tile_localcontextprocessor_pa_t_kernel(
                 nc.sync.dma_start(out=x_tiles[w][:, tiles, :], in_=x_windows[w, :, tiles, :])
                 first += piece
 
-        w_words = keep.tile([P, 2, GROUPS, INNER * PACK], U8, align_bytes=64)
+        w_words = keep.tile([P, 2, GROUPS, INNER * PACK], U8, align_bytes=256)
 
         def load_words(kv, words, half):
             cols = slice(INNER * PACK // 2 * half, INNER * PACK // 2 * (half + 1))
@@ -138,8 +139,11 @@ def tile_localcontextprocessor_pa_t_kernel(
 
         def quantise_x(w, tiles):
             if w not in x_codes:
-                x_codes[w] = twice.tile(
-                    [P, TOKEN_TILES, GROUPS, P], U32, name="x_codes", align_bytes=64
+                shifted = twice.tile(
+                    [P, SHIFT + TOKEN_TILES * GROUPS * P], U32, name="x_codes", align_bytes=256
+                )
+                x_codes[w] = shifted[:, SHIFT:].rearrange(
+                    "p (t g n) -> p t g n", t=TOKEN_TILES, g=GROUPS
                 )
                 x_planes[w] = twice.tile(
                     [P, TOKEN_TILES, GROUPS, P], U8, name="x_planes", align_bytes=64

from contextlib import ExitStack

import concourse.mybir as mybir
from concourse.masks import make_identity

F32 = mybir.dt.float32
BF16 = mybir.dt.bfloat16
I32 = mybir.dt.int32
U32 = mybir.dt.uint32
U8 = mybir.dt.uint8
FP8X4 = mybir.dt.float8_e4m3fn_x4
ACT = mybir.ActivationFunctionType
ALU = mybir.AluOpType

P = 128
PACK = 4
K_PASS = P * PACK

BATCH, TOKENS, FEATURES = 4, 1024, 1024
WINDOW = 512
WINDOWS = BATCH * TOKENS // WINDOW
HEADS, HEAD_DIM = 4, 128
INNER = HEADS * HEAD_DIM
GROUPS = FEATURES // K_PASS
TOKEN_TILES = WINDOW // P
HALVES = 2
HALF_TILES = TOKEN_TILES // HALVES
HALF = HALF_TILES * P
PAIRS = 2
TURNED_TILES = 3
QUADRANTS = 4
SHIFT = 32
WHOLE_RUN = (range(TOKEN_TILES),)
HALF_RUNS = (range(HALF_TILES), range(HALF_TILES, TOKEN_TILES))
K, V = 0, 1

FLOPS = 2 * BATCH * TOKENS * FEATURES * 2 * INNER + 2 * WINDOWS * HEADS * WINDOW * HEAD_DIM * HEAD_DIM


def tile_localcontextprocessor_pa_t_kernel(
    tc, x, w_k_words, w_k_scales, w_v_words, w_v_scales, out
):
    nc = tc.nc
    x_windows = x.rearrange("b (j p t) d -> (b j) p t d", p=P, t=TOKEN_TILES)

    with ExitStack() as ctx:
        ctx.enter_context(tc.manual_schedule())
        keep = ctx.enter_context(tc.tile_pool(name="keep", bufs=1))
        twice = ctx.enter_context(tc.tile_pool(name="twice", bufs=2))
        four = ctx.enter_context(tc.tile_pool(name="four", bufs=4))
        banks = ctx.enter_context(tc.psum_pool(name="banks", bufs=8))

        w_planes = keep.tile([P, 2, GROUPS, INNER], U8, align_bytes=64)
        nc.vector.memset(w_planes[:].bitcast(I32), 0)
        identity = keep.tile([P, P], F32)
        make_identity(nc, identity[:])

        x_tiles = [
            keep.tile([P, TOKEN_TILES, FEATURES], BF16, name="x_win%d" % w) for w in range(WINDOWS)
        ]

        def load_x(w, first, pieces):
            for piece in pieces:
                tiles = slice(first, first + piece)
                nc.sync.dma_start(out=x_tiles[w][:, tiles, :], in_=x_windows[w, :, tiles, :])
                first += piece

        w_words = keep.tile([P, 2, GROUPS, INNER * PACK], U8, align_bytes=256)

        def load_words(kv, words, half):
            cols = slice(INNER * PACK // 2 * half, INNER * PACK // 2 * (half + 1))
            nc.sync.dma_start(
                out=w_words[:, kv, :, cols].bitcast(I32),
                in_=words.rearrange("g p n t -> p g (n t)")[:, :, cols].bitcast(I32),
            )

        def load_scales(kv, scales):
            for quadrant in range(QUADRANTS):
                rows = slice(4 * quadrant, 4 * quadrant + 4)
                nc.sync.dma_start(
                    out=w_planes[32 * quadrant : 32 * quadrant + 4, kv, :, :].bitcast(I32),
                    in_=scales[:, rows, :].rearrange("g r n -> r g n").bitcast(I32),
                )

        load_x(0, 0, (1,))
        load_scales(K, w_k_scales)
        load_x(0, 1, (1, 1, 1))
        load_scales(V, w_v_scales)
        load_words(K, w_k_words, 0)
        load_words(V, w_v_words, 0)
        load_x(1, 0, (2, 2))
        load_words(K, w_k_words, 1)
        load_words(V, w_v_words, 1)
        for w in range(2, WINDOWS):
            load_x(w, 0, (2, 2))

        x_turned, x_grouped, x_codes, x_planes = {}, {}, {}, {}
        kv_grouped, kv_codes, kv_planes = {}, {}, {}

        def turn_x(w, tiles):
            if w not in x_turned:
                x_turned[w] = twice.tile(
                    [P, TURNED_TILES, GROUPS, PAIRS, P], F32, name="x_turned", align_bytes=64
                )
            cut = slice(tiles[0], tiles[-1] + 1)
            nc.vector.tensor_copy(
                out=x_turned[w][:, cut, :, :, :],
                in_=x_tiles[w][:, cut, :]
                .bitcast(F32)
                .rearrange("p t (g n u) -> p t g u n", g=GROUPS, u=PAIRS),
            )

        def transpose_x(w, t, groups):
            x_pairs = x_tiles[w][:].bitcast(F32)
            pairs_in_group = K_PASS // 2
            flipped = banks.tile([P, len(groups), PAIRS, P], F32, tag="bank")
            for i, g in enumerate(groups):
                for u in range(PAIRS):
                    if w in x_turned and t < TURNED_TILES:
                        words = x_turned[w][:, t, g, u, :]
                    else:
                        words = x_pairs[
                            :, t, pairs_in_group * g + u : pairs_in_group * (g + 1) : PAIRS
                        ]
                    nc.tensor.transpose(flipped[:, i, u, :], words, identity[:])
            return flipped

        def group_x(w, t, groups, flipped, copy):
            half = t // HALF_TILES
            if (w, half) not in x_grouped:
                x_grouped[w, half] = four.tile(
                    [P, HALF_TILES, GROUPS, P, PACK], BF16, name="x_grouped", align_bytes=64
                )
            grouped_pairs = x_grouped[w, half][:].bitcast(F32)
            copy(
                out=grouped_pairs[:, t % HALF_TILES, groups[0] : groups[-1] + 1, :, :],
                in_=flipped[:].rearrange("p g u n -> p g n u"),
            )

        def quantise_x(w, tiles):
            if w not in x_codes:
                shifted = twice.tile(
                    [P, SHIFT + TOKEN_TILES * GROUPS * P], U32, name="x_codes", align_bytes=256
                )
                x_codes[w] = shifted[:, SHIFT:].rearrange(
                    "p (t g n) -> p t g n", t=TOKEN_TILES, g=GROUPS
                )
                x_planes[w] = twice.tile(
                    [P, TOKEN_TILES, GROUPS, P], U8, name="x_planes", align_bytes=64
                )
            cut = slice(tiles[0], tiles[-1] + 1)
            cut_in_half = slice(tiles[0] % HALF_TILES, tiles[-1] % HALF_TILES + 1)
            grouped = x_grouped[w, tiles[0] // HALF_TILES]
            nc.vector.quantize_mx(
                out=x_codes[w][:, cut, :, :].rearrange("p t g n -> p (t g n)").bitcast(FP8X4),
                scales=x_planes[w][:, cut, :, :].rearrange("p t g n -> p (t g n)"),
                in_=grouped[:, cut_in_half, :, :, :].rearrange("p t g n k -> p (t g n k)"),
            )

        def project(w, wanted, tile_runs):
            products = {}
            for tiles in tile_runs:
                for kv, h in wanted:
                    if (kv, h) not in products:
                        products[kv, h] = banks.tile(
                            [P, TOKEN_TILES, HEAD_DIM], F32, name="product", tag="bank"
                        )
                    for t in tiles:
                        for g in range(GROUPS):
                            nc.tensor.matmul_mx(
                                out=products[kv, h][:, t, :],
                                lhsT=x_codes[w][:, t, g, :].bitcast(FP8X4),
                                lhsT_scale=x_planes[w][:, t, g, :],
                                rhs=w_words[
                                    :, kv, g, PACK * HEAD_DIM * h : PACK * HEAD_DIM * (h + 1)
                                ].bitcast(FP8X4),
                                rhs_scale=w_planes[:, kv, g, HEAD_DIM * h : HEAD_DIM * (h + 1)],
                                start=(g == 0),
                                stop=(g == GROUPS - 1),
                            )
            return {key: products[key][:].rearrange("p t c -> p c t") for key in wanted}

        def quantise_kv(w, h, first=K, last=V):
            cut = slice(first, last + 1)
            nc.vector.quantize_mx(
                out=kv_codes[w][:, h, cut, :].rearrange("p s c -> p (s c)").bitcast(FP8X4),
                scales=kv_planes[w][:, h, cut, :].rearrange("p s c -> p (s c)"),
                in_=kv_grouped[w][:, h, cut, :, :].rearrange("p s c t -> p (s c t)"),
            )

        def context(w, heads, copy):
            product = banks.tile([P, len(heads), HEAD_DIM], F32, tag="bank")
            for i, h in enumerate(heads):
                nc.tensor.matmul_mx(
                    out=product[:, i, :],
                    lhsT=kv_codes[w][:, h, K, :].bitcast(FP8X4),
                    lhsT_scale=kv_planes[w][:, h, K, :],
                    rhs=kv_codes[w][:, h, V, :].bitcast(FP8X4),
                    rhs_scale=kv_planes[w][:, h, V, :],
                    start=True,
                    stop=True,
                )
            result = four.tile([P, len(heads), HEAD_DIM], F32, name="result")
            copy(out=result[:], in_=product[:])
            nc.sync.dma_start(
                out=out[w, heads[0] : heads[-1] + 1].rearrange("h d e -> d h e"), in_=result[:]
            )

        for t in range(TOKEN_TILES):
            group_x(0, t, range(0, 1), transpose_x(0, t, range(0, 1)), nc.scalar.copy)
            copy = nc.vector.tensor_copy if t == 0 else nc.scalar.copy
            group_x(0, t, range(1, 2), transpose_x(0, t, range(1, 2)), copy)
            if t > 0:
                quantise_x(0, range(t - 1, t))
        quantise_x(0, range(TOKEN_TILES - 1, TOKEN_TILES))

        def exponential(k):
            exp_k = four.tile([P, HEAD_DIM, PACK], BF16, name="exp_k")
            nc.scalar.activation(out=exp_k[:], in_=k, func=ACT.Exp)
            return exp_k

        def clip(exp_k):
            nc.vector.tensor_scalar(
                out=exp_k[:], in0=exp_k[:], scalar1=1.0, scalar2=None, op0=ALU.min
            )

        def finish_kf(w, h, k, exp_k):
            nc.vector.scalar_tensor_tensor(
                out=kv_grouped[w][:, h, K, :, :],
                in0=k,
                scalar=0.0,
                in1=exp_k[:],
                op0=ALU.max,
                op1=ALU.add,
            )

        def group_v(w, h, v):
            nc.scalar.copy(out=kv_grouped[w][:, h, V, :, :], in_=v)

        for w in range(WINDOWS):
            kv_grouped[w] = twice.tile(
                [P, HEADS, 2, HEAD_DIM, PACK], BF16, name="kv_grouped", align_bytes=64
            )
            kv_codes[w] = twice.tile([P, HEADS, 2, HEAD_DIM], U32, name="kv_codes", align_bytes=64)
            kv_planes[w] = twice.tile([P, HEADS, 2, HEAD_DIM], U8, name="kv_planes", align_bytes=64)
            if w == WINDOWS - 1:
                break
            transposing_head = 1 if w == 0 else 0
            for h in range(HEADS):
                if w == 0 and h == 0:
                    k_psum = project(w, ((K, 0), (K, 1)), HALF_RUNS)
                    v_psum = project(w, ((V, 0), (V, 1)), WHOLE_RUN)
                    exps = [exponential(k_psum[K, 0]), exponential(k_psum[K, 1])]
                elif w > 0 or h > 1:
                    k_psum = project(w, ((K, h),), WHOLE_RUN)
                    v_psum = project(w, ((V, h),), WHOLE_RUN)
                    exps = [exponential(k_psum[K, h])]
                exp_k = exps[h if w == 0 and h < 2 else 0]
                group_v(w, h, v_psum[V, h])
                clip(exp_k)
                if h > 0:
                    quantise_kv(w, h - 1)
                elif w > 0:
                    quantise_kv(w - 1, HEADS - 1)
                finish_kf(w, h, k_psum[K, h], exp_k)
                if h == transposing_head:
                    for t in range(TOKEN_TILES):
                        group_x(
                            w + 1,
                            t,
                            range(GROUPS),
                            transpose_x(w + 1, t, range(GROUPS)),
                            nc.scalar.copy,
                        )
                    if w + 2 < WINDOWS:
                        turn_x(w + 2, range(HALF_TILES))
                    quantise_x(w + 1, range(HALF_TILES))
                    if w + 2 < WINDOWS:
                        turn_x(w + 2, range(HALF_TILES, TURNED_TILES))
                    quantise_x(w + 1, range(HALF_TILES, TOKEN_TILES))
                if h == 2 and w > 0:
                    context(w - 1, range(HEADS), nc.vector.tensor_copy if w % 2 else nc.scalar.copy)

        w = WINDOWS - 1
        for h in range(HEADS):
            k = project(w, ((K, h),), WHOLE_RUN)[K, h]
            exp_k = exponential(k)
            clip(exp_k)
            if h == 0:
                quantise_kv(w - 1, HEADS - 1)
            elif h > 1:
                quantise_kv(w, h - 2, K, K)
            finish_kf(w, h, k, exp_k)
        context(w - 1, range(HEADS), nc.scalar.copy)
        for h in (HEADS - 2, HEADS - 1):
            quantise_kv(w, h, K, K)
        for h in range(HEADS):
            group_v(w, h, project(w, ((V, h),), WHOLE_RUN)[V, h])
            quantise_kv(w, h, V, V)
        context(w, range(HEADS - 1), nc.vector.tensor_copy)
        context(w, range(HEADS - 1, HEADS), nc.scalar.copy)
